import numpy as np
import ml_dtypes


def mxq(x, axis, fmt="e4m3"):
    dtype, down = {"e4m3": (ml_dtypes.float8_e4m3fn, 7), "e5m2": (ml_dtypes.float8_e5m2, 14)}[fmt]
    v = np.moveaxis(np.asarray(x, np.float32).astype(ml_dtypes.bfloat16).astype(np.float64), axis, -1)
    blocks = v.reshape(v.shape[:-1] + (-1, 32))
    amax = np.abs(blocks).max(-1, keepdims=True)
    byte = np.maximum(np.where(amax > 0, np.frexp(amax)[1] - 1 + 127, 0) - down, 1)
    scale = np.exp2(byte - 127.0)
    codes = (blocks / scale).astype(np.float32).astype(dtype).astype(np.float64)
    return np.moveaxis((codes * scale).reshape(v.shape), -1, axis)


WIDE = False


def mx_kscale(k):
    if not WIDE:
        return np.ones(k)
    levels = np.array([10, -10, 5, -5, 0])
    if k % 512:
        return np.exp2(np.random.permutation(np.resize(levels, k // 32))).repeat(32)
    a = np.empty((k // 512, 16))
    for p in range(k // 512):
        a[p, :8] = np.random.permutation(np.resize(levels, 8))
        for g in range(8):
            far = levels[np.abs(levels - a[p, g]) >= 10]
            a[p, g + 8] = far[np.random.randint(len(far))]
    return np.exp2(a.ravel()).repeat(32)


BF16 = ml_dtypes.bfloat16


def bf(x):
    return np.asarray(x, np.float32).astype(BF16)


def f64(x):
    return np.asarray(x).astype(np.float64)


B, IN, HID, N, NM = 64, 2, 62, 512, 5
C = IN + HID


def setup_inputs():
    s = mx_kscale(N)
    return {"x": bf(np.random.standard_normal((B, C, N)) * s),
            "support0": bf(np.random.standard_normal((N, N)) * 0.7 / np.sqrt(N) * s[:, None] / s[None, :]),
            "support1": bf(np.random.standard_normal((N, N)) * 0.7 / np.sqrt(N) * s[:, None] / s[None, :])}


def reference(x, support0, support1):
    x0 = f64(x)
    xq = mxq(x0, 2, "e4m3")
    a0q = mxq(f64(support0).T, 0, "e4m3")
    a1q = mxq(f64(support1).T, 0, "e4m3")
    x1_0 = xq @ a0q
    x2_0 = 2.0 * (mxq(x1_0, 2, "e4m3") @ a0q) - x0
    x1_1 = xq @ a1q
    x2_1 = 2.0 * (mxq(x1_1, 2, "e4m3") @ a1q) - x0
    return np.concatenate([x1_0, x2_0, x1_1, x2_1], axis=1)

@@ -1,0 +1,248 @@
+from contextlib import ExitStack
+
+import concourse.mybir as mybir
+from concourse.masks import make_identity
+
+F32 = mybir.dt.float32
+BF16 = mybir.dt.bfloat16
+U32 = mybir.dt.uint32
+U8 = mybir.dt.uint8
+FP8X4 = mybir.dt.float8_e4m3fn_x4
+MULT = mybir.AluOpType.mult
+SUBTRACT = mybir.AluOpType.subtract
+
+P = 128
+NODES = 512
+FLOPS = 4 * 2 * 4096 * 512 * 512
+
+QUADS = 8
+UNITS = 8
+STEPS = 8 * UNITS
+LAG = 3
+STAGE_BUFS = 7
+MID_TILES = 4
+VECTOR_E1 = 4
+
+
+def tile_dcgrucell_pa_t_kernel(tc, x, support0, support1, out):
+    nc = tc.nc
+    supports = (support0, support1)
+    x_v = x.flatten_outer_dims().rearrange(
+        "(s p q e) n -> s q p (e n)", s=2, p=P, q=4, e=4
+    )
+    out_v = out.rearrange("(s b) (k j e) n -> s k b j (e n)", b=32, k=4, j=4, e=16)
+
+    with ExitStack() as ctx:
+        keep = ctx.enter_context(tc.tile_pool(name="keep", bufs=1))
+        grp = ctx.enter_context(tc.tile_pool(name="grp", bufs=4))
+        stp = ctx.enter_context(tc.tile_pool(name="stp", bufs=LAG + 2))
+        stage = ctx.enter_context(tc.tile_pool(name="stage", bufs=STAGE_BUFS))
+        psum = ctx.enter_context(tc.psum_pool(name="psum", bufs=2))
+        ctx.enter_context(tc.manual_schedule())
+
+        a_raw = []
+        xq = []
+        for a in range(2):
+            a_raw.append(keep.tile([P, 4 * NODES], BF16, name="a_raw%d" % a, tag="a_raw%d" % a))
+        for quad in range(QUADS):
+            xq.append(keep.tile([P, 4 * NODES], BF16, name="xq%d" % quad, tag="xq%d" % quad))
+
+        def load_a(a):
+            nc.sync.dma_start(
+                out=a_raw[a][:],
+                in_=supports[a].rearrange("(p t) n -> p (t n)", t=4),
+            )
+
+        def load_x(quad):
+            nc.sync.dma_start(out=xq[quad][:], in_=x_v[quad // 4, quad % 4])
+
+        load_x(0)
+        load_a(0)
+        load_x(1)
+        load_a(1)
+        for quad in range(2, QUADS):
+            load_x(quad)
+
+        ident = keep.tile([P, P], F32, name="ident", tag="ident")
+        make_identity(nc, ident[:])
+
+        def vcopy(o, i):
+            nc.vector.tensor_copy(out=o, in_=i)
+
+        def scopy(o, i):
+            nc.scalar.copy(out=o, in_=i)
+
+        def transposes(src, pair, tag):
+            words = src[:].bitcast(F32).rearrange("p (c w) -> p c w", c=4)
+            bank = psum.tile([P, 512], F32, name="tr", tag=tag)
+            for u in range(2):
+                for ee in range(2):
+                    col = (2 * u + ee) * P
+                    nc.tensor.transpose(
+                        bank[:, col : col + P],
+                        words[:, 2 * pair + ee, u : 2 * P : 2],
+                        ident[:],
+                    )
+            return bank
+
+        def evac_same_order(copy, bank, grouped, half):
+            copy(
+                grouped[:].bitcast(F32)[:, half * 512 : (half + 1) * 512].rearrange(
+                    "w (c u) -> w c u", u=2
+                ),
+                bank[:].rearrange("w (u c) -> w c u", u=2),
+            )
+
+        def evac_natural(copy, bank, grouped, half):
+            copy(
+                grouped[:].bitcast(F32).rearrange(
+                    "w (p h e u) -> w h p e u", h=2, e=2, u=2
+                )[:, half],
+                bank[:].rearrange("w (u e p) -> w p e u", u=2, e=2),
+            )
+
+        def quantise(grouped, codes, scales):
+            nc.vector.quantize_mx(out=codes.bitcast(FP8X4), scales=scales, in_=grouped)
+
+        an_c, an_s, ap_c, ap_s = [], [], [], []
+        for a in range(2):
+            an_c.append(keep.tile([P, NODES], U32, name="an_c%d" % a, tag="an_c%d" % a, align_bytes=64))
+            an_s.append(keep.tile([P, NODES], U8, name="an_s%d" % a, tag="an_s%d" % a, align_bytes=64))
+            ap_c.append(keep.tile([P, NODES], U32, name="ap_c%d" % a, tag="ap_c%d" % a, align_bytes=64))
+            ap_s.append(keep.tile([P, NODES], U8, name="ap_s%d" % a, tag="ap_s%d" % a, align_bytes=64))
+        xc, xs = [], []
+        for quad in range(QUADS):
+            xc.append(keep.tile([P, 512], U32, name="xc%d" % quad, tag="xc%d" % quad, align_bytes=64))
+            xs.append(keep.tile([P, 512], U8, name="xs%d" % quad, tag="xs%d" % quad, align_bytes=64))
+
+        abank, gp, gn, xbank, gx = {}, {}, {}, {}, {}
+
+        def prep_a_pe(a, tag):
+            abank[a] = [transposes(a_raw[a], 0, tag), transposes(a_raw[a], 1, tag)]
+            gp[a] = grp.tile([P, 2048], BF16, name="gp", tag="grp", align_bytes=64)
+            gn[a] = grp.tile([P, 2048], BF16, name="gn", tag="grp", align_bytes=64)
+
+        def prep_a_evac(a, half, copy):
+            evac_same_order(copy, abank[a][half], gp[a], half)
+            evac_natural(copy, abank[a][half], gn[a], half)
+
+        def prep_a_quant(a):
+            quantise(gp[a][:], ap_c[a][:], ap_s[a][:])
+            quantise(gn[a][:], an_c[a][:], an_s[a][:])
+
+        def prep_x_pe(quad, tag):
+            xbank[quad] = [transposes(xq[quad], 0, tag), transposes(xq[quad], 1, tag)]
+            gx[quad] = grp.tile([P, 2048], BF16, name="gx", tag="grp", align_bytes=64)
+
+        def prep_x_evac(quad, half, copy):
+            evac_same_order(copy, xbank[quad][half], gx[quad], half)
+
+        def prep_x_quant(quad):
+            quantise(gx[quad][:], xc[quad][:], xs[quad][:])
+
+        prep_x_pe(0, "tr")
+        prep_a_pe(0, "x2")
+        prep_x_pe(1, "x1")
+        prep_x_evac(0, 0, vcopy)
+        prep_x_evac(0, 1, scopy)
+        prep_x_quant(0)
+        prep_a_evac(0, 0, vcopy)
+        prep_a_evac(0, 1, scopy)
+        prep_a_quant(0)
+        prep_x_evac(1, 0, scopy)
+        prep_x_evac(1, 1, scopy)
+
+        x_prep_step = {}
+        for quad in range(2, QUADS):
+            x_prep_step[8 * (quad - 2) + 6] = quad
+
+        def mx(o, lc, ls, rc, rs):
+            nc.tensor.matmul_mx(
+                out=o,
+                lhsT=lc.bitcast(FP8X4),
+                lhsT_scale=ls,
+                rhs=rc.bitcast(FP8X4),
+                rhs_scale=rs,
+                start=True,
+                stop=True,
+            )
+
+        def where(step):
+            unit, e8 = step // 8, step % 8
+            e16 = 8 * ((unit // 2) % 2) + e8
+            return unit, e8, unit % 2, 4 * (unit // 4) + e16 // 4, e16 % 4
+
+        staged = {}
+
+        def staging(kind, unit, e8):
+            if e8 == 0:
+                staged[kind] = stage.tile([P, 8 * NODES], F32, name="st%d" % kind, tag="st")
+            return staged[kind][:, e8 * NODES : (e8 + 1) * NODES]
+
+        def store_if_full(kind, unit, e8):
+            dst = out_v[unit // 4, 2 * (unit % 2) + kind]
+            e0 = 8 * ((unit // 2) % 2)
+            if (e8 + 1) % MID_TILES == 0:
+                first = e8 + 1 - MID_TILES
+                here = slice(first * NODES, (e8 + 1) * NODES)
+                there = slice((e0 + first) * NODES, (e0 + e8 + 1) * NODES)
+                nc.sync.dma_start(out=dst[8:24, :, there], in_=staged[kind][32:96, here])
+            if e8 == 7:
+                there = slice(e0 * NODES, (e0 + 8) * NODES)
+                nc.gpsimd.dma_start(out=dst[0:8, :, there], in_=staged[kind][0:32, :])
+                nc.gpsimd.dma_start(out=dst[24:32, :, there], in_=staged[kind][96:128, :])
+
+        c1 = {}
+        s1 = {}
+        for j in range(STEPS + LAG):
+            if j < STEPS:
+                unit, e8, a, quad, e4 = where(j)
+                cols = slice(e4 * P, (e4 + 1) * P)
+                t1 = psum.tile([P, 512], F32, name="t1", tag="t1")
+                for t in range(4):
+                    chunk = slice(t * P, (t + 1) * P)
+                    mx(t1[:, chunk], ap_c[a][:, chunk], ap_s[a][:, chunk], xc[quad][:, cols], xs[quad][:, cols])
+                b1 = psum.tile([P, 512], F32, name="b1", tag="x1")
+                mx(b1[:], xc[quad][:, cols], xs[quad][:, cols], an_c[a][:], an_s[a][:])
+                g1 = stp.tile([P, 512], BF16, name="g1", tag="g1", align_bytes=64)
+                copy = vcopy if j % 8 == VECTOR_E1 else scopy
+                copy(
+                    g1[:].rearrange("p (r t) -> p r t", t=4),
+                    t1[:].rearrange("p (t r) -> p r t", t=4),
+                )
+                scopy(staging(0, unit, e8), b1[:])
+                store_if_full(0, unit, e8)
+            i = j - LAG
+            if i >= 0:
+                unit, e8, a, quad, e4 = where(i)
+                b2 = psum.tile([P, 512], F32, name="b2", tag="x2")
+                mx(b2[:], c1[i][:], s1[i][:], an_c[a][:], an_s[a][:])
+                nc.vector.scalar_tensor_tensor(
+                    out=staging(1, unit, e8),
+                    in0=b2[:],
+                    scalar=2.0,
+                    in1=xq[quad][:, e4 * NODES : (e4 + 1) * NODES],
+                    op0=MULT,
+                    op1=SUBTRACT,
+                )
+                store_if_full(1, unit, e8)
+            if j < STEPS:
+                c1[j] = stp.tile([P, P], U32, name="c1", tag="c1", align_bytes=64)
+                s1[j] = stp.tile([P, P], U8, name="s1", tag="s1", align_bytes=64)
+                quantise(g1[:], c1[j][:], s1[j][:])
+            if j == 0:
+                prep_x_quant(1)
+            if j in x_prep_step:
+                prep_x_pe(x_prep_step[j], "tr")
+                prep_x_evac(x_prep_step[j], 0, vcopy)
+            if j - 1 in x_prep_step:
+                prep_x_evac(x_prep_step[j - 1], 1, vcopy)
+            if j - 2 in x_prep_step:
+                prep_x_quant(x_prep_step[j - 2])
+            if j == 2:
+                prep_a_pe(1, "tr")
+                prep_a_evac(1, 0, vcopy)
+            if j == 3:
+                prep_a_evac(1, 1, scopy)
+            if j == 5:
+                prep_a_quant(1)

@@ -186,11 +186,7 @@ def tile_dcgrucell_pa_t_kernel(tc, x, support0, support1, out):
                 first = e8 + 1 - MID_TILES
                 here = slice(first * NODES, (e8 + 1) * NODES)
                 there = slice((e0 + first) * NODES, (e0 + e8 + 1) * NODES)
-                nc.sync.dma_start(out=dst[8:24, :, there], in_=staged[kind][32:96, here])
-            if e8 == 7:
-                there = slice(e0 * NODES, (e0 + 8) * NODES)
-                nc.gpsimd.dma_start(out=dst[0:8, :, there], in_=staged[kind][0:32, :])
-                nc.gpsimd.dma_start(out=dst[24:32, :, there], in_=staged[kind][96:128, :])
+                nc.sync.dma_start(out=dst[:, :, there], in_=staged[kind][:, here])
 
         c1 = {}
         s1 = {}

@@ -182,7 +182,11 @@ def tile_dcgrucell_pa_t_kernel(tc, x, support0, support1, out):
         def store_if_full(kind, unit, e8):
             dst = out_v[unit // 4, 2 * (unit % 2) + kind]
             e0 = 8 * ((unit // 2) % 2)
-            if (e8 + 1) % MID_TILES == 0:
+            if unit == UNITS - 1 and e8 >= 8 - MID_TILES:
+                here = slice(e8 * NODES, (e8 + 1) * NODES)
+                there = slice((e0 + e8) * NODES, (e0 + e8 + 1) * NODES)
+                nc.sync.dma_start(out=dst[:, :, there], in_=staged[kind][:, here])
+            elif (e8 + 1) % MID_TILES == 0:
                 first = e8 + 1 - MID_TILES
                 here = slice(first * NODES, (e8 + 1) * NODES)
                 there = slice((e0 + first) * NODES, (e0 + e8 + 1) * NODES)

@@ -56,8 +56,10 @@ def tile_dcgrucell_pa_t_kernel(tc, x, support0, support1, out):
         def load_x(quad):
             nc.sync.dma_start(out=xq[quad][:], in_=x_v[quad // 4, quad % 4])
 
-        load_x(0)
         load_a(0)
+        for half in range(2):
+            cols = slice(half * 2 * NODES, (half + 1) * 2 * NODES)
+            nc.sync.dma_start(out=xq[0][:, cols], in_=x_v[0, 0][:, cols])
         load_x(1)
         load_a(1)
         for quad in range(2, QUADS):
@@ -93,21 +95,11 @@ def tile_dcgrucell_pa_t_kernel(tc, x, support0, support1, out):
                 bank[:].rearrange("w (u c) -> w c u", u=2),
             )
 
-        def evac_natural(copy, bank, grouped, half):
-            copy(
-                grouped[:].bitcast(F32).rearrange(
-                    "w (p h e u) -> w h p e u", h=2, e=2, u=2
-                )[:, half],
-                bank[:].rearrange("w (u e p) -> w p e u", u=2, e=2),
-            )
-
         def quantise(grouped, codes, scales):
             nc.vector.quantize_mx(out=codes.bitcast(FP8X4), scales=scales, in_=grouped)
 
-        an_c, an_s, ap_c, ap_s = [], [], [], []
+        ap_c, ap_s = [], []
         for a in range(2):
-            an_c.append(keep.tile([P, NODES], U32, name="an_c%d" % a, tag="an_c%d" % a, align_bytes=64))
-            an_s.append(keep.tile([P, NODES], U8, name="an_s%d" % a, tag="an_s%d" % a, align_bytes=64))
             ap_c.append(keep.tile([P, NODES], U32, name="ap_c%d" % a, tag="ap_c%d" % a, align_bytes=64))
             ap_s.append(keep.tile([P, NODES], U8, name="ap_s%d" % a, tag="ap_s%d" % a, align_bytes=64))
         xc, xs = [], []
@@ -115,20 +107,17 @@ def tile_dcgrucell_pa_t_kernel(tc, x, support0, support1, out):
             xc.append(keep.tile([P, 512], U32, name="xc%d" % quad, tag="xc%d" % quad, align_bytes=64))
             xs.append(keep.tile([P, 512], U8, name="xs%d" % quad, tag="xs%d" % quad, align_bytes=64))
 
-        abank, gp, gn, xbank, gx = {}, {}, {}, {}, {}
+        abank, gp, xbank, gx = {}, {}, {}, {}
 
         def prep_a_pe(a, tag):
             abank[a] = [transposes(a_raw[a], 0, tag), transposes(a_raw[a], 1, tag)]
             gp[a] = grp.tile([P, 2048], BF16, name="gp", tag="grp", align_bytes=64)
-            gn[a] = grp.tile([P, 2048], BF16, name="gn", tag="grp", align_bytes=64)
 
         def prep_a_evac(a, half, copy):
             evac_same_order(copy, abank[a][half], gp[a], half)
-            evac_natural(copy, abank[a][half], gn[a], half)
 
         def prep_a_quant(a):
             quantise(gp[a][:], ap_c[a][:], ap_s[a][:])
-            quantise(gn[a][:], an_c[a][:], an_s[a][:])
 
         def prep_x_pe(quad, tag):
             xbank[quad] = [transposes(xq[quad], 0, tag), transposes(xq[quad], 1, tag)]
@@ -140,17 +129,23 @@ def tile_dcgrucell_pa_t_kernel(tc, x, support0, support1, out):
         def prep_x_quant(quad):
             quantise(gx[quad][:], xc[quad][:], xs[quad][:])
 
-        prep_x_pe(0, "tr")
+        def quant_half(grouped, codes, scales, half):
+            quantise(
+                grouped[:, half * 1024 : (half + 1) * 1024],
+                codes[:, half * 256 : (half + 1) * 256],
+                scales[:, half * 256 : (half + 1) * 256],
+            )
+
         prep_a_pe(0, "x2")
-        prep_x_pe(1, "x1")
-        prep_x_evac(0, 0, vcopy)
-        prep_x_evac(0, 1, scopy)
-        prep_x_quant(0)
+        prep_x_pe(0, "tr")
         prep_a_evac(0, 0, vcopy)
         prep_a_evac(0, 1, scopy)
-        prep_a_quant(0)
-        prep_x_evac(1, 0, scopy)
-        prep_x_evac(1, 1, scopy)
+        quant_half(gp[0], ap_c[0], ap_s[0], 0)
+        prep_x_evac(0, 0, scopy)
+        quant_half(gp[0], ap_c[0], ap_s[0], 1)
+        prep_x_evac(0, 1, scopy)
+        quant_half(gx[0], xc[0], xs[0], 0)
+        quant_half(gx[0], xc[0], xs[0], 1)
 
         x_prep_step = {}
         for quad in range(2, QUADS):
@@ -192,6 +187,12 @@ def tile_dcgrucell_pa_t_kernel(tc, x, support0, support1, out):
                 there = slice((e0 + first) * NODES, (e0 + e8 + 1) * NODES)
                 nc.sync.dma_start(out=dst[:, :, there], in_=staged[kind][:, here])
 
+        def natural(ap):
+            return ap.rearrange("r (j t) -> r j t", t=4)
+
+        def permuted(ap):
+            return ap.rearrange("r (t j) -> r j t", t=4)
+
         c1 = {}
         s1 = {}
         for j in range(STEPS + LAG):
@@ -203,25 +204,25 @@ def tile_dcgrucell_pa_t_kernel(tc, x, support0, support1, out):
                     chunk = slice(t * P, (t + 1) * P)
                     mx(t1[:, chunk], ap_c[a][:, chunk], ap_s[a][:, chunk], xc[quad][:, cols], xs[quad][:, cols])
                 b1 = psum.tile([P, 512], F32, name="b1", tag="x1")
-                mx(b1[:], xc[quad][:, cols], xs[quad][:, cols], an_c[a][:], an_s[a][:])
+                mx(b1[:], xc[quad][:, cols], xs[quad][:, cols], ap_c[a][:], ap_s[a][:])
                 g1 = stp.tile([P, 512], BF16, name="g1", tag="g1", align_bytes=64)
                 copy = vcopy if j % 8 == VECTOR_E1 else scopy
                 copy(
                     g1[:].rearrange("p (r t) -> p r t", t=4),
                     t1[:].rearrange("p (t r) -> p r t", t=4),
                 )
-                scopy(staging(0, unit, e8), b1[:])
+                scopy(natural(staging(0, unit, e8)), permuted(b1[:]))
                 store_if_full(0, unit, e8)
             i = j - LAG
             if i >= 0:
                 unit, e8, a, quad, e4 = where(i)
                 b2 = psum.tile([P, 512], F32, name="b2", tag="x2")
-                mx(b2[:], c1[i][:], s1[i][:], an_c[a][:], an_s[a][:])
+                mx(b2[:], c1[i][:], s1[i][:], ap_c[a][:], ap_s[a][:])
                 nc.vector.scalar_tensor_tensor(
-                    out=staging(1, unit, e8),
-                    in0=b2[:],
+                    out=natural(staging(1, unit, e8)),
+                    in0=permuted(b2[:]),
                     scalar=2.0,
-                    in1=xq[quad][:, e4 * NODES : (e4 + 1) * NODES],
+                    in1=natural(xq[quad][:, e4 * NODES : (e4 + 1) * NODES]),
                     op0=MULT,
                     op1=SUBTRACT,
                 )
@@ -231,6 +232,12 @@ def tile_dcgrucell_pa_t_kernel(tc, x, support0, support1, out):
                 s1[j] = stp.tile([P, P], U8, name="s1", tag="s1", align_bytes=64)
                 quantise(g1[:], c1[j][:], s1[j][:])
             if j == 0:
+                gx[1] = grp.tile([P, 2048], BF16, name="gx", tag="grp", align_bytes=64)
+                xbank[1] = {}
+            if j < 2:
+                xbank[1][j] = transposes(xq[1], j, "x2")
+                prep_x_evac(1, j, vcopy)
+            if j == 2:
                 prep_x_quant(1)
             if j in x_prep_step:
                 prep_x_pe(x_prep_step[j], "tr")

@@ -9,6 +9,7 @@ U32 = mybir.dt.uint32
 U8 = mybir.dt.uint8
 FP8X4 = mybir.dt.float8_e4m3fn_x4
 MULT = mybir.AluOpType.mult
+ADD = mybir.AluOpType.add
 SUBTRACT = mybir.AluOpType.subtract
 
 P = 128
@@ -16,12 +17,8 @@ NODES = 512
 FLOPS = 4 * 2 * 4096 * 512 * 512
 
 QUADS = 8
-UNITS = 8
-STEPS = 8 * UNITS
-LAG = 3
-STAGE_BUFS = 7
-MID_TILES = 4
-VECTOR_E1 = 4
+BLOCKS = 16
+STAGE_BUFS = 14
 
 
 def tile_dcgrucell_pa_t_kernel(tc, x, support0, support1, out):
@@ -30,14 +27,18 @@ def tile_dcgrucell_pa_t_kernel(tc, x, support0, support1, out):
     x_v = x.flatten_outer_dims().rearrange(
         "(s p q e) n -> s q p (e n)", s=2, p=P, q=4, e=4
     )
-    out_v = out.rearrange("(s b) (k j e) n -> s k b j (e n)", b=32, k=4, j=4, e=16)
+    out_v = out.rearrange("(s b) (k j q e) n -> s k q b j (e n)", b=32, k=4, j=4, q=4, e=4)
 
     with ExitStack() as ctx:
         keep = ctx.enter_context(tc.tile_pool(name="keep", bufs=1))
-        grp = ctx.enter_context(tc.tile_pool(name="grp", bufs=4))
-        stp = ctx.enter_context(tc.tile_pool(name="stp", bufs=LAG + 2))
+        grp = ctx.enter_context(tc.tile_pool(name="grp", bufs=3))
+        hp = ctx.enter_context(tc.tile_pool(name="hp", bufs=4))
+        gp = ctx.enter_context(tc.tile_pool(name="gp", bufs=2))
+        cp = ctx.enter_context(tc.tile_pool(name="cp", bufs=2))
         stage = ctx.enter_context(tc.tile_pool(name="stage", bufs=STAGE_BUFS))
-        psum = ctx.enter_context(tc.psum_pool(name="psum", bufs=2))
+        ps_first = ctx.enter_context(tc.psum_pool(name="ps_first", bufs=4))
+        ps_second = ctx.enter_context(tc.psum_pool(name="ps_second", bufs=2))
+        ps_tr = ctx.enter_context(tc.psum_pool(name="ps_tr", bufs=2))
         ctx.enter_context(tc.manual_schedule())
 
         a_raw = []
@@ -47,23 +48,16 @@ def tile_dcgrucell_pa_t_kernel(tc, x, support0, support1, out):
         for quad in range(QUADS):
             xq.append(keep.tile([P, 4 * NODES], BF16, name="xq%d" % quad, tag="xq%d" % quad))
 
-        def load_a(a):
-            nc.sync.dma_start(
-                out=a_raw[a][:],
-                in_=supports[a].rearrange("(p t) n -> p (t n)", t=4),
-            )
+        def a_view(a):
+            return supports[a].rearrange("(p t) n -> p (t n)", t=4)
 
-        def load_x(quad):
+        for src, dst in ((a_view(0), a_raw[0]), (x_v[0, 0], xq[0])):
+            for half in range(2):
+                cols = slice(half * 2 * NODES, (half + 1) * 2 * NODES)
+                nc.sync.dma_start(out=dst[:, cols], in_=src[:, cols])
+        nc.sync.dma_start(out=a_raw[1][:], in_=a_view(1))
+        for quad in range(1, QUADS):
             nc.sync.dma_start(out=xq[quad][:], in_=x_v[quad // 4, quad % 4])
-
-        load_a(0)
-        for half in range(2):
-            cols = slice(half * 2 * NODES, (half + 1) * 2 * NODES)
-            nc.sync.dma_start(out=xq[0][:, cols], in_=x_v[0, 0][:, cols])
-        load_x(1)
-        load_a(1)
-        for quad in range(2, QUADS):
-            load_x(quad)
 
         ident = keep.tile([P, P], F32, name="ident", tag="ident")
         make_identity(nc, ident[:])
@@ -74,82 +68,63 @@ def tile_dcgrucell_pa_t_kernel(tc, x, support0, support1, out):
         def scopy(o, i):
             nc.scalar.copy(out=o, in_=i)
 
-        def transposes(src, pair, tag):
-            words = src[:].bitcast(F32).rearrange("p (c w) -> p c w", c=4)
-            bank = psum.tile([P, 512], F32, name="tr", tag=tag)
-            for u in range(2):
-                for ee in range(2):
-                    col = (2 * u + ee) * P
-                    nc.tensor.transpose(
-                        bank[:, col : col + P],
-                        words[:, 2 * pair + ee, u : 2 * P : 2],
-                        ident[:],
-                    )
-            return bank
-
-        def evac_same_order(copy, bank, grouped, half):
-            copy(
-                grouped[:].bitcast(F32)[:, half * 512 : (half + 1) * 512].rearrange(
-                    "w (c u) -> w c u", u=2
-                ),
-                bank[:].rearrange("w (u c) -> w c u", u=2),
-            )
-
         def quantise(grouped, codes, scales):
             nc.vector.quantize_mx(out=codes.bitcast(FP8X4), scales=scales, in_=grouped)
 
-        ap_c, ap_s = [], []
+        a_c, a_s = [], []
         for a in range(2):
-            ap_c.append(keep.tile([P, NODES], U32, name="ap_c%d" % a, tag="ap_c%d" % a, align_bytes=64))
-            ap_s.append(keep.tile([P, NODES], U8, name="ap_s%d" % a, tag="ap_s%d" % a, align_bytes=64))
+            a_c.append(keep.tile([P, NODES], U32, name="a_c%d" % a, tag="a_c%d" % a, align_bytes=64))
+            a_s.append(keep.tile([P, NODES], U8, name="a_s%d" % a, tag="a_s%d" % a, align_bytes=64))
         xc, xs = [], []
         for quad in range(QUADS):
             xc.append(keep.tile([P, 512], U32, name="xc%d" % quad, tag="xc%d" % quad, align_bytes=64))
             xs.append(keep.tile([P, 512], U8, name="xs%d" % quad, tag="xs%d" % quad, align_bytes=64))
 
-        abank, gp, xbank, gx = {}, {}, {}, {}
+        bank_of, grouped_of = {}, {}
 
-        def prep_a_pe(a, tag):
-            abank[a] = [transposes(a_raw[a], 0, tag), transposes(a_raw[a], 1, tag)]
-            gp[a] = grp.tile([P, 2048], BF16, name="gp", tag="grp", align_bytes=64)
+        def job_pe(job, half, pool):
+            src = a_raw[job[1]] if job[0] == "a" else xq[job[1]]
+            words = src[:].bitcast(F32).rearrange("p (c w) -> p c w", c=4)
+            bank = pool.tile([P, 512], F32, name="bank", tag="bank")
+            for u in range(2):
+                for ee in range(2):
+                    col = (2 * u + ee) * P
+                    nc.tensor.transpose(
+                        bank[:, col : col + P], words[:, 2 * half + ee, u : 2 * P : 2], ident[:]
+                    )
+            bank_of[(job, half)] = bank
+            if half == 0:
+                grouped_of[job] = grp.tile([P, 2048], BF16, name="grouped", tag="grp", align_bytes=64)
 
-        def prep_a_evac(a, half, copy):
-            evac_same_order(copy, abank[a][half], gp[a], half)
-
-        def prep_a_quant(a):
-            quantise(gp[a][:], ap_c[a][:], ap_s[a][:])
-
-        def prep_x_pe(quad, tag):
-            xbank[quad] = [transposes(xq[quad], 0, tag), transposes(xq[quad], 1, tag)]
-            gx[quad] = grp.tile([P, 2048], BF16, name="gx", tag="grp", align_bytes=64)
-
-        def prep_x_evac(quad, half, copy):
-            evac_same_order(copy, xbank[quad][half], gx[quad], half)
-
-        def prep_x_quant(quad):
-            quantise(gx[quad][:], xc[quad][:], xs[quad][:])
-
-        def quant_half(grouped, codes, scales, half):
-            quantise(
-                grouped[:, half * 1024 : (half + 1) * 1024],
-                codes[:, half * 256 : (half + 1) * 256],
-                scales[:, half * 256 : (half + 1) * 256],
+        def job_evac(job, half, copy):
+            copy(
+                grouped_of[job][:].bitcast(F32)[:, half * 512 : (half + 1) * 512].rearrange(
+                    "w (c u) -> w c u", u=2
+                ),
+                bank_of[(job, half)][:].rearrange("w (u c) -> w c u", u=2),
             )
 
-        prep_a_pe(0, "x2")
-        prep_x_pe(0, "tr")
-        prep_a_evac(0, 0, vcopy)
-        prep_a_evac(0, 1, scopy)
-        quant_half(gp[0], ap_c[0], ap_s[0], 0)
-        prep_x_evac(0, 0, scopy)
-        quant_half(gp[0], ap_c[0], ap_s[0], 1)
-        prep_x_evac(0, 1, scopy)
-        quant_half(gx[0], xc[0], xs[0], 0)
-        quant_half(gx[0], xc[0], xs[0], 1)
+        def job_quant(job, halves):
+            codes, scales = (a_c, a_s) if job[0] == "a" else (xc, xs)
+            lo, hi = halves[0], halves[-1] + 1
+            quantise(
+                grouped_of[job][:, lo * 1024 : hi * 1024],
+                codes[job[1]][:, lo * 256 : hi * 256],
+                scales[job[1]][:, lo * 256 : hi * 256],
+            )
 
-        x_prep_step = {}
-        for quad in range(2, QUADS):
-            x_prep_step[8 * (quad - 2) + 6] = quad
+        for half in range(2):
+            job_pe(("a", 0), half, ps_tr)
+        for half in range(2):
+            job_pe(("x", 0), half, ps_second)
+        job_evac(("a", 0), 0, vcopy)
+        job_evac(("a", 0), 1, scopy)
+        job_quant(("a", 0), (0,))
+        job_evac(("x", 0), 0, scopy)
+        job_quant(("a", 0), (1,))
+        job_evac(("x", 0), 1, scopy)
+        job_quant(("x", 0), (0,))
+        job_quant(("x", 0), (1,))
 
         def mx(o, lc, ls, rc, rs):
             nc.tensor.matmul_mx(
@@ -162,30 +137,24 @@ def tile_dcgrucell_pa_t_kernel(tc, x, support0, support1, out):
                 stop=True,
             )
 
-        def where(step):
-            unit, e8 = step // 8, step % 8
-            e16 = 8 * ((unit // 2) % 2) + e8
-            return unit, e8, unit % 2, 4 * (unit // 4) + e16 // 4, e16 % 4
-
         staged = {}
 
-        def staging(kind, unit, e8):
-            if e8 == 0:
-                staged[kind] = stage.tile([P, 8 * NODES], F32, name="st%d" % kind, tag="st")
-            return staged[kind][:, e8 * NODES : (e8 + 1) * NODES]
+        def staging(kind, g, s):
+            if (kind, g) not in staged:
+                staged[(kind, g)] = stage.tile([P, 4 * NODES], F32, name="st%d" % kind, tag="st")
+            return staged[(kind, g)][:, s * NODES : (s + 1) * NODES]
 
-        def store_if_full(kind, unit, e8):
-            dst = out_v[unit // 4, 2 * (unit % 2) + kind]
-            e0 = 8 * ((unit // 2) % 2)
-            if unit == UNITS - 1 and e8 >= 8 - MID_TILES:
-                here = slice(e8 * NODES, (e8 + 1) * NODES)
-                there = slice((e0 + e8) * NODES, (e0 + e8 + 1) * NODES)
-                nc.sync.dma_start(out=dst[:, :, there], in_=staged[kind][:, here])
-            elif (e8 + 1) % MID_TILES == 0:
-                first = e8 + 1 - MID_TILES
-                here = slice(first * NODES, (e8 + 1) * NODES)
-                there = slice((e0 + first) * NODES, (e0 + e8 + 1) * NODES)
-                nc.sync.dma_start(out=dst[:, :, there], in_=staged[kind][:, here])
+        done = {}
+
+        def store(kind, g, s):
+            quad, a = g // 2, g % 2
+            dst = out_v[quad // 4, 2 * a + kind, quad % 4]
+            done[(kind, g)] = done.get((kind, g), 0) + 1
+            if g == BLOCKS - 1:
+                cols = slice(s * NODES, (s + 1) * NODES)
+                nc.sync.dma_start(out=dst[:, :, cols], in_=staged[(kind, g)][:, cols])
+            elif done[(kind, g)] == 4:
+                nc.sync.dma_start(out=dst, in_=staged[(kind, g)][:])
 
         def natural(ap):
             return ap.rearrange("r (j t) -> r j t", t=4)
@@ -193,63 +162,132 @@ def tile_dcgrucell_pa_t_kernel(tc, x, support0, support1, out):
         def permuted(ap):
             return ap.rearrange("r (t j) -> r j t", t=4)
 
-        c1 = {}
-        s1 = {}
-        for j in range(STEPS + LAG):
-            if j < STEPS:
-                unit, e8, a, quad, e4 = where(j)
-                cols = slice(e4 * P, (e4 + 1) * P)
-                t1 = psum.tile([P, 512], F32, name="t1", tag="t1")
-                for t in range(4):
-                    chunk = slice(t * P, (t + 1) * P)
-                    mx(t1[:, chunk], ap_c[a][:, chunk], ap_s[a][:, chunk], xc[quad][:, cols], xs[quad][:, cols])
-                b1 = psum.tile([P, 512], F32, name="b1", tag="x1")
-                mx(b1[:], xc[quad][:, cols], xs[quad][:, cols], ap_c[a][:], ap_s[a][:])
-                g1 = stp.tile([P, 512], BF16, name="g1", tag="g1", align_bytes=64)
-                copy = vcopy if j % 8 == VECTOR_E1 else scopy
-                copy(
-                    g1[:].rearrange("p (r t) -> p r t", t=4),
-                    t1[:].rearrange("p (t r) -> p r t", t=4),
+        h, tr_of, g_m, g_t, c_m, s_m, c_t, s_t = {}, {}, {}, {}, {}, {}, {}, {}
+
+        def first_product(g, s):
+            quad, a = g // 2, g % 2
+            cols = slice(s * P, (s + 1) * P)
+            b1 = ps_first.tile([P, 512], F32, name="b1", tag="bank")
+            mx(b1[:], xc[quad][:, cols], xs[quad][:, cols], a_c[a][:], a_s[a][:])
+            return b1
+
+        def transposed_product(g, s):
+            quad, a = g // 2, g % 2
+            cols = slice(s * P, (s + 1) * P)
+            t1 = ps_first.tile([P, 512], F32, name="t1", tag="bank")
+            for t in range(4):
+                chunk = slice(t * P, (t + 1) * P)
+                mx(t1[:, chunk], a_c[a][:, chunk], a_s[a][:, chunk], xc[quad][:, cols], xs[quad][:, cols])
+            return t1
+
+        def x1_out(g, s, b1):
+            dst = staging(0, g, s)
+            scopy(natural(dst), permuted(b1[:]))
+            store(0, g, s)
+            return dst
+
+        def second_products(g, steps):
+            quad, a = g // 2, g % 2
+            banks = {}
+            for s in steps:
+                codes, scales = (c_t[g], s_t[g]) if s < 2 else (c_m[g], s_m[g])
+                rows = slice((s % 2) * P, (s % 2 + 1) * P)
+                banks[s] = ps_second.tile([P, 512], F32, name="b2", tag="bank")
+                mx(banks[s][:], codes[:, rows], scales[:, rows], a_c[a][:], a_s[a][:])
+            return banks
+
+        def x2_out(g, s, b2):
+            quad = g // 2
+            nc.vector.scalar_tensor_tensor(
+                out=natural(staging(1, g, s)),
+                in0=permuted(b2[:]),
+                scalar=2.0,
+                in1=natural(xq[quad][:, s * NODES : (s + 1) * NODES]),
+                op0=MULT,
+                op1=SUBTRACT,
+            )
+            store(1, g, s)
+
+        half_at = {}
+        for quad in range(2, QUADS):
+            for half in range(2):
+                half_at[2 * quad - 3 + half] = (("x", quad), half)
+
+        for g in range(BLOCKS + 1):
+            cur, prev = g < BLOCKS, g >= 1
+            if prev:
+                g_t[g - 1] = gp.tile([P, 2 * NODES], BF16, name="g_t", tag="g_t", align_bytes=64)
+                scopy(
+                    g_t[g - 1][:].bitcast(F32).rearrange("p (jj r u) -> p jj r u", jj=2, u=2),
+                    tr_of[g - 1][:].rearrange("p (jj u r) -> p jj r u", jj=2, u=2),
                 )
-                scopy(natural(staging(0, unit, e8)), permuted(b1[:]))
-                store_if_full(0, unit, e8)
-            i = j - LAG
-            if i >= 0:
-                unit, e8, a, quad, e4 = where(i)
-                b2 = psum.tile([P, 512], F32, name="b2", tag="x2")
-                mx(b2[:], c1[i][:], s1[i][:], ap_c[a][:], ap_s[a][:])
-                nc.vector.scalar_tensor_tensor(
-                    out=natural(staging(1, unit, e8)),
-                    in0=permuted(b2[:]),
-                    scalar=2.0,
-                    in1=natural(xq[quad][:, e4 * NODES : (e4 + 1) * NODES]),
-                    op0=MULT,
-                    op1=SUBTRACT,
-                )
-                store_if_full(1, unit, e8)
-            if j < STEPS:
-                c1[j] = stp.tile([P, P], U32, name="c1", tag="c1", align_bytes=64)
-                s1[j] = stp.tile([P, P], U8, name="s1", tag="s1", align_bytes=64)
-                quantise(g1[:], c1[j][:], s1[j][:])
-            if j == 0:
-                gx[1] = grp.tile([P, 2048], BF16, name="gx", tag="grp", align_bytes=64)
-                xbank[1] = {}
-            if j < 2:
-                xbank[1][j] = transposes(xq[1], j, "x2")
-                prep_x_evac(1, j, vcopy)
-            if j == 2:
-                prep_x_quant(1)
-            if j in x_prep_step:
-                prep_x_pe(x_prep_step[j], "tr")
-                prep_x_evac(x_prep_step[j], 0, vcopy)
-            if j - 1 in x_prep_step:
-                prep_x_evac(x_prep_step[j - 1], 1, vcopy)
-            if j - 2 in x_prep_step:
-                prep_x_quant(x_prep_step[j - 2])
-            if j == 2:
-                prep_a_pe(1, "tr")
-                prep_a_evac(1, 0, vcopy)
-            if j == 3:
-                prep_a_evac(1, 1, scopy)
-            if j == 5:
-                prep_a_quant(1)
+                c_m[g - 1] = cp.tile([P, 2 * P], U32, name="c_m", tag="c_m", align_bytes=64)
+                s_m[g - 1] = cp.tile([P, 2 * P], U8, name="s_m", tag="s_m", align_bytes=64)
+                quantise(g_m[g - 1][:], c_m[g - 1][:], s_m[g - 1][:])
+            if g == 1:
+                job_evac(("x", 1), 1, vcopy)
+            if g - 1 in half_at:
+                job, half = half_at[g - 1]
+                job_evac(job, half, vcopy)
+            if prev:
+                c_t[g - 1] = cp.tile([P, 2 * P], U32, name="c_t", tag="c_t", align_bytes=64)
+                s_t[g - 1] = cp.tile([P, 2 * P], U8, name="s_t", tag="s_t", align_bytes=64)
+                quantise(g_t[g - 1][:], c_t[g - 1][:], s_t[g - 1][:])
+            if g - 1 in half_at and half_at[g - 1][1] == 1:
+                job_quant(half_at[g - 1][0], (0, 1))
+            if cur:
+                banks = [first_product(g, 0), first_product(g, 1)]
+                for s in range(2):
+                    dst = x1_out(g, s, banks[s])
+                    h[(g, s)] = hp.tile([P, NODES], BF16, name="h", tag="h")
+                    nc.gpsimd.tensor_scalar(
+                        out=h[(g, s)][:].rearrange("r (u p e) -> r u p e", u=2, e=2),
+                        in0=dst.rearrange("r (p u e) -> r u p e", u=2, e=2),
+                        scalar1=1.0,
+                        scalar2=0.0,
+                        op0=MULT,
+                        op1=ADD,
+                    )
+            if cur:
+                g_m[g] = gp.tile([P, 2 * NODES], BF16, name="g_m", tag="g_m", align_bytes=64)
+            for s in (2, 3):
+                if cur:
+                    b1 = first_product(g, s)
+                    t1 = transposed_product(g, s)
+                if g == 0 and s == 2:
+                    for half in range(2):
+                        job_pe(("a", 1), half, ps_second)
+                    job_pe(("x", 1), 0, ps_tr)
+                    job_evac(("a", 1), 0, vcopy)
+                    job_evac(("a", 1), 1, vcopy)
+                    job_quant(("a", 1), (0, 1))
+                    job_evac(("x", 1), 0, vcopy)
+                if prev:
+                    steps = (2, 3) if s == 2 else (0, 1)
+                    b2 = second_products(g - 1, steps)
+                if cur:
+                    x1_out(g, s, b1)
+                    scopy(
+                        g_m[g][:, (s - 2) * 512 : (s - 1) * 512].rearrange("p (r t) -> p r t", t=4),
+                        t1[:].rearrange("p (t r) -> p r t", t=4),
+                    )
+                if prev:
+                    for k in steps:
+                        x2_out(g - 1, k, b2[k])
+                if g == 1 and s == 2:
+                    job_quant(("x", 1), (0, 1))
+            if cur:
+                tr_of[g] = ps_tr.tile([P, 512], F32, name="tr", tag="bank")
+                for jj in range(2):
+                    for u in range(2):
+                        col = (2 * jj + u) * P
+                        nc.tensor.transpose(
+                            tr_of[g][:, col : col + P],
+                            h[(g, jj)][:].bitcast(F32)[:, u * P : (u + 1) * P],
+                            ident[:],
+                        )
+            if g == 0:
+                job_pe(("x", 1), 1, ps_second)
+            if g in half_at:
+                job, half = half_at[g]
+                job_pe(job, half, ps_tr)

@@ -19,14 +19,13 @@ FLOPS = 4 * 2 * 4096 * 512 * 512
 QUADS = 8
 BLOCKS = 16
 STAGE_BUFS = 14
+EARLY_BLOCKS = 2
 
 
 def tile_dcgrucell_pa_t_kernel(tc, x, support0, support1, out):
     nc = tc.nc
     supports = (support0, support1)
-    x_v = x.flatten_outer_dims().rearrange(
-        "(s p q e) n -> s q p (e n)", s=2, p=P, q=4, e=4
-    )
+    x_v = x.flatten_outer_dims().rearrange("(s p r) n -> s p (r n)", s=2, p=P, r=16)
     out_v = out.rearrange("(s b) (k j q e) n -> s k q b j (e n)", b=32, k=4, j=4, q=4, e=4)
 
     with ExitStack() as ctx:
@@ -42,22 +41,31 @@ def tile_dcgrucell_pa_t_kernel(tc, x, support0, support1, out):
         ctx.enter_context(tc.manual_schedule())
 
         a_raw = []
-        xq = []
+        x_half = []
         for a in range(2):
             a_raw.append(keep.tile([P, 4 * NODES], BF16, name="a_raw%d" % a, tag="a_raw%d" % a))
-        for quad in range(QUADS):
-            xq.append(keep.tile([P, 4 * NODES], BF16, name="xq%d" % quad, tag="xq%d" % quad))
+        for s in range(2):
+            x_half.append(keep.tile([P, 16 * NODES], BF16, name="x_half%d" % s, tag="x_half%d" % s))
+
+        def xq(quad):
+            return x_half[quad // 4][:, (quad % 4) * 4 * NODES : (quad % 4 + 1) * 4 * NODES]
+
+        def load_x(s, first, rows):
+            cols = slice(first * NODES, (first + rows) * NODES)
+            nc.sync.dma_start(out=x_half[s][:, cols], in_=x_v[s][:, cols])
 
         def a_view(a):
             return supports[a].rearrange("(p t) n -> p (t n)", t=4)
 
-        for src, dst in ((a_view(0), a_raw[0]), (x_v[0, 0], xq[0])):
-            for half in range(2):
-                cols = slice(half * 2 * NODES, (half + 1) * 2 * NODES)
-                nc.sync.dma_start(out=dst[:, cols], in_=src[:, cols])
+        for half in range(2):
+            cols = slice(half * 2 * NODES, (half + 1) * 2 * NODES)
+            nc.sync.dma_start(out=a_raw[0][:, cols], in_=a_view(0)[:, cols])
+        load_x(0, 0, 2)
+        load_x(0, 2, 2)
         nc.sync.dma_start(out=a_raw[1][:], in_=a_view(1))
-        for quad in range(1, QUADS):
-            nc.sync.dma_start(out=xq[quad][:], in_=x_v[quad // 4, quad % 4])
+        load_x(0, 4, 4)
+        load_x(0, 8, 8)
+        load_x(1, 0, 16)
 
         ident = keep.tile([P, P], F32, name="ident", tag="ident")
         make_identity(nc, ident[:])
@@ -83,8 +91,8 @@ def tile_dcgrucell_pa_t_kernel(tc, x, support0, support1, out):
         bank_of, grouped_of = {}, {}
 
         def job_pe(job, half, pool):
-            src = a_raw[job[1]] if job[0] == "a" else xq[job[1]]
-            words = src[:].bitcast(F32).rearrange("p (c w) -> p c w", c=4)
+            src = a_raw[job[1]][:] if job[0] == "a" else xq(job[1])
+            words = src.bitcast(F32).rearrange("p (c w) -> p c w", c=4)
             bank = pool.tile([P, 512], F32, name="bank", tag="bank")
             for u in range(2):
                 for ee in range(2):
@@ -150,9 +158,10 @@ def tile_dcgrucell_pa_t_kernel(tc, x, support0, support1, out):
             quad, a = g // 2, g % 2
             dst = out_v[quad // 4, 2 * a + kind, quad % 4]
             done[(kind, g)] = done.get((kind, g), 0) + 1
-            if g == BLOCKS - 1:
-                cols = slice(s * NODES, (s + 1) * NODES)
-                nc.sync.dma_start(out=dst[:, :, cols], in_=staged[(kind, g)][:, cols])
+            if g < EARLY_BLOCKS or (g == BLOCKS - 1 and kind == 1):
+                if done[(kind, g)] % 2 == 0:
+                    cols = slice((s // 2) * 2 * NODES, (s // 2 + 1) * 2 * NODES)
+                    nc.sync.dma_start(out=dst[:, :, cols], in_=staged[(kind, g)][:, cols])
             elif done[(kind, g)] == 4:
                 nc.sync.dma_start(out=dst, in_=staged[(kind, g)][:])
 
@@ -202,7 +211,7 @@ def tile_dcgrucell_pa_t_kernel(tc, x, support0, support1, out):
                 out=natural(staging(1, g, s)),
                 in0=permuted(b2[:]),
                 scalar=2.0,
-                in1=natural(xq[quad][:, s * NODES : (s + 1) * NODES]),
+                in1=natural(xq(quad)[:, s * NODES : (s + 1) * NODES]),
                 op0=MULT,
                 op1=SUBTRACT,
             )

@@ -247,16 +247,16 @@ def tile_dcgrucell_pa_t_kernel(tc, x, support0, support1, out):
             if cur:
                 banks = [first_product(g, 0), first_product(g, 1)]
                 for s in range(2):
-                    dst = x1_out(g, s, banks[s])
-                    h[(g, s)] = hp.tile([P, NODES], BF16, name="h", tag="h")
-                    nc.gpsimd.tensor_scalar(
-                        out=h[(g, s)][:].rearrange("r (u p e) -> r u p e", u=2, e=2),
-                        in0=dst.rearrange("r (p u e) -> r u p e", u=2, e=2),
-                        scalar1=1.0,
-                        scalar2=0.0,
-                        op0=MULT,
-                        op1=ADD,
-                    )
+                    x1_out(g, s, banks[s])
+                h[g] = hp.tile([P, 2 * NODES], BF16, name="h", tag="h")
+                nc.gpsimd.tensor_scalar(
+                    out=h[g][:].rearrange("r (u p e) -> r u p e", u=2, e=2),
+                    in0=staged[(0, g)][:, 0 : 2 * NODES].rearrange("r (p u e) -> r u p e", u=2, e=2),
+                    scalar1=1.0,
+                    scalar2=0.0,
+                    op0=MULT,
+                    op1=ADD,
+                )
             if cur:
                 g_m[g] = gp.tile([P, 2 * NODES], BF16, name="g_m", tag="g_m", align_bytes=64)
             for s in (2, 3):
@@ -292,7 +292,7 @@ def tile_dcgrucell_pa_t_kernel(tc, x, support0, support1, out):
                         col = (2 * jj + u) * P
                         nc.tensor.transpose(
                             tr_of[g][:, col : col + P],
-                            h[(g, jj)][:].bitcast(F32)[:, u * P : (u + 1) * P],
+                            h[g][:].bitcast(F32)[:, (2 * u + jj) * P : (2 * u + jj + 1) * P],
                             ident[:],
                         )
             if g == 0:

@@ -25,8 +25,8 @@ EARLY_BLOCKS = 2
 def tile_dcgrucell_pa_t_kernel(tc, x, support0, support1, out):
     nc = tc.nc
     supports = (support0, support1)
-    x_v = x.flatten_outer_dims().rearrange("(s p r) n -> s p (r n)", s=2, p=P, r=16)
-    out_v = out.rearrange("(s b) (k j q e) n -> s k q b j (e n)", b=32, k=4, j=4, q=4, e=4)
+    x_v = x.flatten_outer_dims().rearrange("(p r) n -> p (r n)", p=P, r=32)
+    out_v = out.rearrange("b (k j q e) n -> q k b j (e n)", k=4, j=2, q=8, e=4)
 
     with ExitStack() as ctx:
         keep = ctx.enter_context(tc.tile_pool(name="keep", bufs=1))
@@ -41,18 +41,16 @@ def tile_dcgrucell_pa_t_kernel(tc, x, support0, support1, out):
         ctx.enter_context(tc.manual_schedule())
 
         a_raw = []
-        x_half = []
         for a in range(2):
             a_raw.append(keep.tile([P, 4 * NODES], BF16, name="a_raw%d" % a, tag="a_raw%d" % a))
-        for s in range(2):
-            x_half.append(keep.tile([P, 16 * NODES], BF16, name="x_half%d" % s, tag="x_half%d" % s))
+        x_raw = keep.tile([P, 32 * NODES], BF16, name="x_raw", tag="x_raw")
 
         def xq(quad):
-            return x_half[quad // 4][:, (quad % 4) * 4 * NODES : (quad % 4 + 1) * 4 * NODES]
+            return x_raw[:, quad * 4 * NODES : (quad + 1) * 4 * NODES]
 
-        def load_x(s, first, rows):
+        def load_x(first, rows):
             cols = slice(first * NODES, (first + rows) * NODES)
-            nc.sync.dma_start(out=x_half[s][:, cols], in_=x_v[s][:, cols])
+            nc.sync.dma_start(out=x_raw[:, cols], in_=x_v[:, cols])
 
         def a_view(a):
             return supports[a].rearrange("(p t) n -> p (t n)", t=4)
@@ -60,12 +58,12 @@ def tile_dcgrucell_pa_t_kernel(tc, x, support0, support1, out):
         for half in range(2):
             cols = slice(half * 2 * NODES, (half + 1) * 2 * NODES)
             nc.sync.dma_start(out=a_raw[0][:, cols], in_=a_view(0)[:, cols])
-        load_x(0, 0, 2)
-        load_x(0, 2, 2)
+        load_x(0, 2)
+        load_x(2, 2)
         nc.sync.dma_start(out=a_raw[1][:], in_=a_view(1))
-        load_x(0, 4, 4)
-        load_x(0, 8, 8)
-        load_x(1, 0, 16)
+        load_x(4, 4)
+        load_x(8, 8)
+        load_x(16, 16)
 
         ident = keep.tile([P, P], F32, name="ident", tag="ident")
         make_identity(nc, ident[:])
@@ -156,7 +154,7 @@ def tile_dcgrucell_pa_t_kernel(tc, x, support0, support1, out):
 
         def store(kind, g, s):
             quad, a = g // 2, g % 2
-            dst = out_v[quad // 4, 2 * a + kind, quad % 4]
+            dst = out_v[quad, 2 * a + kind]
             done[(kind, g)] = done.get((kind, g), 0) + 1
             if g < EARLY_BLOCKS or (g == BLOCKS - 1 and kind == 1):
                 if done[(kind, g)] % 2 == 0:

@@ -62,8 +62,7 @@ def tile_dcgrucell_pa_t_kernel(tc, x, support0, support1, out):
         load_x(2, 2)
         nc.sync.dma_start(out=a_raw[1][:], in_=a_view(1))
         load_x(4, 4)
-        load_x(8, 8)
-        load_x(16, 16)
+        load_x(8, 24)
 
         ident = keep.tile([P, P], F32, name="ident", tag="ident")
         make_identity(nc, ident[:])
@@ -119,10 +118,21 @@ def tile_dcgrucell_pa_t_kernel(tc, x, support0, support1, out):
                 scales[job[1]][:, lo * 256 : hi * 256],
             )
 
+        warm = keep.tile([P, 512], BF16, name="warm", tag="warm")
+        nc.vector.memset(warm[:], 0.0)
+
+        def warm_up(count):
+            for i in range(count):
+                bank = ps_first.tile([P, 512], F32, name="warm_out", tag="bank")
+                nc.tensor.matmul(bank[:], lhsT=warm[:, 0:P], rhs=warm[:], start=True, stop=True)
+
+        warm_up(4)
         for half in range(2):
             job_pe(("a", 0), half, ps_tr)
+        warm_up(1)
         for half in range(2):
             job_pe(("x", 0), half, ps_second)
+        warm_up(2)
         job_evac(("a", 0), 0, vcopy)
         job_evac(("a", 0), 1, scopy)
         job_quant(("a", 0), (0,))
@@ -156,7 +166,7 @@ def tile_dcgrucell_pa_t_kernel(tc, x, support0, support1, out):
             quad, a = g // 2, g % 2
             dst = out_v[quad, 2 * a + kind]
             done[(kind, g)] = done.get((kind, g), 0) + 1
-            if g < EARLY_BLOCKS or (g == BLOCKS - 1 and kind == 1):
+            if g < EARLY_BLOCKS:
                 if done[(kind, g)] % 2 == 0:
                     cols = slice((s // 2) * 2 * NODES, (s // 2 + 1) * 2 * NODES)
                     nc.sync.dma_start(out=dst[:, :, cols], in_=staged[(kind, g)][:, cols])
@@ -189,7 +199,8 @@ def tile_dcgrucell_pa_t_kernel(tc, x, support0, support1, out):
 
         def x1_out(g, s, b1):
             dst = staging(0, g, s)
-            scopy(natural(dst), permuted(b1[:]))
+            copy = vcopy if g == 0 and s == 1 else scopy
+            copy(natural(dst), permuted(b1[:]))
             store(0, g, s)
             return dst
 
@@ -240,8 +251,6 @@ def tile_dcgrucell_pa_t_kernel(tc, x, support0, support1, out):
                 c_t[g - 1] = cp.tile([P, 2 * P], U32, name="c_t", tag="c_t", align_bytes=64)
                 s_t[g - 1] = cp.tile([P, 2 * P], U8, name="s_t", tag="s_t", align_bytes=64)
                 quantise(g_t[g - 1][:], c_t[g - 1][:], s_t[g - 1][:])
-            if g - 1 in half_at and half_at[g - 1][1] == 1:
-                job_quant(half_at[g - 1][0], (0, 1))
             if cur:
                 banks = [first_product(g, 0), first_product(g, 1)]
                 for s in range(2):
@@ -283,6 +292,8 @@ def tile_dcgrucell_pa_t_kernel(tc, x, support0, support1, out):
                         x2_out(g - 1, k, b2[k])
                 if g == 1 and s == 2:
                     job_quant(("x", 1), (0, 1))
+                if s == 2 and g - 1 in half_at and half_at[g - 1][1] == 1:
+                    job_quant(half_at[g - 1][0], (0, 1))
             if cur:
                 tr_of[g] = ps_tr.tile([P, 512], F32, name="tr", tag="bank")
                 for jj in range(2):

@@ -19,7 +19,7 @@ FLOPS = 4 * 2 * 4096 * 512 * 512
 QUADS = 8
 BLOCKS = 16
 STAGE_BUFS = 14
-EARLY_BLOCKS = 2
+EARLY_BLOCKS = 3
 
 
 def tile_dcgrucell_pa_t_kernel(tc, x, support0, support1, out):

from contextlib import ExitStack

import concourse.mybir as mybir
from concourse.masks import make_identity

F32 = mybir.dt.float32
BF16 = mybir.dt.bfloat16
U32 = mybir.dt.uint32
U8 = mybir.dt.uint8
FP8X4 = mybir.dt.float8_e4m3fn_x4
MULT = mybir.AluOpType.mult
ADD = mybir.AluOpType.add
SUBTRACT = mybir.AluOpType.subtract

P = 128
NODES = 512
FLOPS = 4 * 2 * 4096 * 512 * 512

QUADS = 8
BLOCKS = 16
STAGE_BUFS = 14
EARLY_BLOCKS = 3


def tile_dcgrucell_pa_t_kernel(tc, x, support0, support1, out):
    nc = tc.nc
    supports = (support0, support1)
    x_v = x.flatten_outer_dims().rearrange("(p r) n -> p (r n)", p=P, r=32)
    out_v = out.rearrange("b (k j q e) n -> q k b j (e n)", k=4, j=2, q=8, e=4)

    with ExitStack() as ctx:
        keep = ctx.enter_context(tc.tile_pool(name="keep", bufs=1))
        grp = ctx.enter_context(tc.tile_pool(name="grp", bufs=3))
        hp = ctx.enter_context(tc.tile_pool(name="hp", bufs=4))
        gp = ctx.enter_context(tc.tile_pool(name="gp", bufs=2))
        cp = ctx.enter_context(tc.tile_pool(name="cp", bufs=2))
        stage = ctx.enter_context(tc.tile_pool(name="stage", bufs=STAGE_BUFS))
        ps_first = ctx.enter_context(tc.psum_pool(name="ps_first", bufs=4))
        ps_second = ctx.enter_context(tc.psum_pool(name="ps_second", bufs=2))
        ps_tr = ctx.enter_context(tc.psum_pool(name="ps_tr", bufs=2))
        ctx.enter_context(tc.manual_schedule())

        a_raw = []
        for a in range(2):
            a_raw.append(keep.tile([P, 4 * NODES], BF16, name="a_raw%d" % a, tag="a_raw%d" % a))
        x_raw = keep.tile([P, 32 * NODES], BF16, name="x_raw", tag="x_raw")

        def xq(quad):
            return x_raw[:, quad * 4 * NODES : (quad + 1) * 4 * NODES]

        def load_x(first, rows):
            cols = slice(first * NODES, (first + rows) * NODES)
            nc.sync.dma_start(out=x_raw[:, cols], in_=x_v[:, cols])

        def a_view(a):
            return supports[a].rearrange("(p t) n -> p (t n)", t=4)

        for half in range(2):
            cols = slice(half * 2 * NODES, (half + 1) * 2 * NODES)
            nc.sync.dma_start(out=a_raw[0][:, cols], in_=a_view(0)[:, cols])
        load_x(0, 2)
        load_x(2, 2)
        nc.sync.dma_start(out=a_raw[1][:], in_=a_view(1))
        load_x(4, 4)
        load_x(8, 24)

        ident = keep.tile([P, P], F32, name="ident", tag="ident")
        make_identity(nc, ident[:])

        def vcopy(o, i):
            nc.vector.tensor_copy(out=o, in_=i)

        def scopy(o, i):
            nc.scalar.copy(out=o, in_=i)

        def quantise(grouped, codes, scales):
            nc.vector.quantize_mx(out=codes.bitcast(FP8X4), scales=scales, in_=grouped)

        a_c, a_s = [], []
        for a in range(2):
            a_c.append(keep.tile([P, NODES], U32, name="a_c%d" % a, tag="a_c%d" % a, align_bytes=64))
            a_s.append(keep.tile([P, NODES], U8, name="a_s%d" % a, tag="a_s%d" % a, align_bytes=64))
        xc, xs = [], []
        for quad in range(QUADS):
            xc.append(keep.tile([P, 512], U32, name="xc%d" % quad, tag="xc%d" % quad, align_bytes=64))
            xs.append(keep.tile([P, 512], U8, name="xs%d" % quad, tag="xs%d" % quad, align_bytes=64))

        bank_of, grouped_of = {}, {}

        def job_pe(job, half, pool):
            src = a_raw[job[1]][:] if job[0] == "a" else xq(job[1])
            words = src.bitcast(F32).rearrange("p (c w) -> p c w", c=4)
            bank = pool.tile([P, 512], F32, name="bank", tag="bank")
            for u in range(2):
                for ee in range(2):
                    col = (2 * u + ee) * P
                    nc.tensor.transpose(
                        bank[:, col : col + P], words[:, 2 * half + ee, u : 2 * P : 2], ident[:]
                    )
            bank_of[(job, half)] = bank
            if half == 0:
                grouped_of[job] = grp.tile([P, 2048], BF16, name="grouped", tag="grp", align_bytes=64)

        def job_evac(job, half, copy):
            copy(
                grouped_of[job][:].bitcast(F32)[:, half * 512 : (half + 1) * 512].rearrange(
                    "w (c u) -> w c u", u=2
                ),
                bank_of[(job, half)][:].rearrange("w (u c) -> w c u", u=2),
            )

        def job_quant(job, halves):
            codes, scales = (a_c, a_s) if job[0] == "a" else (xc, xs)
            lo, hi = halves[0], halves[-1] + 1
            quantise(
                grouped_of[job][:, lo * 1024 : hi * 1024],
                codes[job[1]][:, lo * 256 : hi * 256],
                scales[job[1]][:, lo * 256 : hi * 256],
            )

        warm = keep.tile([P, 512], BF16, name="warm", tag="warm")
        nc.vector.memset(warm[:], 0.0)

        def warm_up(count):
            for i in range(count):
                bank = ps_first.tile([P, 512], F32, name="warm_out", tag="bank")
                nc.tensor.matmul(bank[:], lhsT=warm[:, 0:P], rhs=warm[:], start=True, stop=True)

        warm_up(4)
        for half in range(2):
            job_pe(("a", 0), half, ps_tr)
        warm_up(1)
        for half in range(2):
            job_pe(("x", 0), half, ps_second)
        warm_up(2)
        job_evac(("a", 0), 0, vcopy)
        job_evac(("a", 0), 1, scopy)
        job_quant(("a", 0), (0,))
        job_evac(("x", 0), 0, scopy)
        job_quant(("a", 0), (1,))
        job_evac(("x", 0), 1, scopy)
        job_quant(("x", 0), (0,))
        job_quant(("x", 0), (1,))

        def mx(o, lc, ls, rc, rs):
            nc.tensor.matmul_mx(
                out=o,
                lhsT=lc.bitcast(FP8X4),
                lhsT_scale=ls,
                rhs=rc.bitcast(FP8X4),
                rhs_scale=rs,
                start=True,
                stop=True,
            )

        staged = {}

        def staging(kind, g, s):
            if (kind, g) not in staged:
                staged[(kind, g)] = stage.tile([P, 4 * NODES], F32, name="st%d" % kind, tag="st")
            return staged[(kind, g)][:, s * NODES : (s + 1) * NODES]

        done = {}

        def store(kind, g, s):
            quad, a = g // 2, g % 2
            dst = out_v[quad, 2 * a + kind]
            done[(kind, g)] = done.get((kind, g), 0) + 1
            if g < EARLY_BLOCKS:
                if done[(kind, g)] % 2 == 0:
                    cols = slice((s // 2) * 2 * NODES, (s // 2 + 1) * 2 * NODES)
                    nc.sync.dma_start(out=dst[:, :, cols], in_=staged[(kind, g)][:, cols])
            elif done[(kind, g)] == 4:
                nc.sync.dma_start(out=dst, in_=staged[(kind, g)][:])

        def natural(ap):
            return ap.rearrange("r (j t) -> r j t", t=4)

        def permuted(ap):
            return ap.rearrange("r (t j) -> r j t", t=4)

        h, tr_of, g_m, g_t, c_m, s_m, c_t, s_t = {}, {}, {}, {}, {}, {}, {}, {}

        def first_product(g, s):
            quad, a = g // 2, g % 2
            cols = slice(s * P, (s + 1) * P)
            b1 = ps_first.tile([P, 512], F32, name="b1", tag="bank")
            mx(b1[:], xc[quad][:, cols], xs[quad][:, cols], a_c[a][:], a_s[a][:])
            return b1

        def transposed_product(g, s):
            quad, a = g // 2, g % 2
            cols = slice(s * P, (s + 1) * P)
            t1 = ps_first.tile([P, 512], F32, name="t1", tag="bank")
            for t in range(4):
                chunk = slice(t * P, (t + 1) * P)
                mx(t1[:, chunk], a_c[a][:, chunk], a_s[a][:, chunk], xc[quad][:, cols], xs[quad][:, cols])
            return t1

        def x1_out(g, s, b1):
            dst = staging(0, g, s)
            copy = vcopy if g == 0 and s == 1 else scopy
            copy(natural(dst), permuted(b1[:]))
            store(0, g, s)
            return dst

        def second_products(g, steps):
            quad, a = g // 2, g % 2
            banks = {}
            for s in steps:
                codes, scales = (c_t[g], s_t[g]) if s < 2 else (c_m[g], s_m[g])
                rows = slice((s % 2) * P, (s % 2 + 1) * P)
                banks[s] = ps_second.tile([P, 512], F32, name="b2", tag="bank")
                mx(banks[s][:], codes[:, rows], scales[:, rows], a_c[a][:], a_s[a][:])
            return banks

        def x2_out(g, s, b2):
            quad = g // 2
            nc.vector.scalar_tensor_tensor(
                out=natural(staging(1, g, s)),
                in0=permuted(b2[:]),
                scalar=2.0,
                in1=natural(xq(quad)[:, s * NODES : (s + 1) * NODES]),
                op0=MULT,
                op1=SUBTRACT,
            )
            store(1, g, s)

        half_at = {}
        for quad in range(2, QUADS):
            for half in range(2):
                half_at[2 * quad - 3 + half] = (("x", quad), half)

        for g in range(BLOCKS + 1):
            cur, prev = g < BLOCKS, g >= 1
            if prev:
                g_t[g - 1] = gp.tile([P, 2 * NODES], BF16, name="g_t", tag="g_t", align_bytes=64)
                scopy(
                    g_t[g - 1][:].bitcast(F32).rearrange("p (jj r u) -> p jj r u", jj=2, u=2),
                    tr_of[g - 1][:].rearrange("p (jj u r) -> p jj r u", jj=2, u=2),
                )
                c_m[g - 1] = cp.tile([P, 2 * P], U32, name="c_m", tag="c_m", align_bytes=64)
                s_m[g - 1] = cp.tile([P, 2 * P], U8, name="s_m", tag="s_m", align_bytes=64)
                quantise(g_m[g - 1][:], c_m[g - 1][:], s_m[g - 1][:])
            if g == 1:
                job_evac(("x", 1), 1, vcopy)
            if g - 1 in half_at:
                job, half = half_at[g - 1]
                job_evac(job, half, vcopy)
            if prev:
                c_t[g - 1] = cp.tile([P, 2 * P], U32, name="c_t", tag="c_t", align_bytes=64)
                s_t[g - 1] = cp.tile([P, 2 * P], U8, name="s_t", tag="s_t", align_bytes=64)
                quantise(g_t[g - 1][:], c_t[g - 1][:], s_t[g - 1][:])
            if cur:
                banks = [first_product(g, 0), first_product(g, 1)]
                for s in range(2):
                    x1_out(g, s, banks[s])
                h[g] = hp.tile([P, 2 * NODES], BF16, name="h", tag="h")
                nc.gpsimd.tensor_scalar(
                    out=h[g][:].rearrange("r (u p e) -> r u p e", u=2, e=2),
                    in0=staged[(0, g)][:, 0 : 2 * NODES].rearrange("r (p u e) -> r u p e", u=2, e=2),
                    scalar1=1.0,
                    scalar2=0.0,
                    op0=MULT,
                    op1=ADD,
                )
            if cur:
                g_m[g] = gp.tile([P, 2 * NODES], BF16, name="g_m", tag="g_m", align_bytes=64)
            for s in (2, 3):
                if cur:
                    b1 = first_product(g, s)
                    t1 = transposed_product(g, s)
                if g == 0 and s == 2:
                    for half in range(2):
                        job_pe(("a", 1), half, ps_second)
                    job_pe(("x", 1), 0, ps_tr)
                    job_evac(("a", 1), 0, vcopy)
                    job_evac(("a", 1), 1, vcopy)
                    job_quant(("a", 1), (0, 1))
                    job_evac(("x", 1), 0, vcopy)
                if prev:
                    steps = (2, 3) if s == 2 else (0, 1)
                    b2 = second_products(g - 1, steps)
                if cur:
                    x1_out(g, s, b1)
                    scopy(
                        g_m[g][:, (s - 2) * 512 : (s - 1) * 512].rearrange("p (r t) -> p r t", t=4),
                        t1[:].rearrange("p (t r) -> p r t", t=4),
                    )
                if prev:
                    for k in steps:
                        x2_out(g - 1, k, b2[k])
                if g == 1 and s == 2:
                    job_quant(("x", 1), (0, 1))
                if s == 2 and g - 1 in half_at and half_at[g - 1][1] == 1:
                    job_quant(half_at[g - 1][0], (0, 1))
            if cur:
                tr_of[g] = ps_tr.tile([P, 512], F32, name="tr", tag="bank")
                for jj in range(2):
                    for u in range(2):
                        col = (2 * jj + u) * P
                        nc.tensor.transpose(
                            tr_of[g][:, col : col + P],
                            h[g][:].bitcast(F32)[:, (2 * u + jj) * P : (2 * u + jj + 1) * P],
                            ident[:],
                        )
            if g == 0:
                job_pe(("x", 1), 1, ps_second)
            if g in half_at:
                job, half = half_at[g]
                job_pe(job, half, ps_tr)
